import numpy as np
import ml_dtypes


def mxq(x, axis, fmt="e4m3"):
    dtype, down = {"e4m3": (ml_dtypes.float8_e4m3fn, 7), "e5m2": (ml_dtypes.float8_e5m2, 14)}[fmt]
    v = np.moveaxis(np.asarray(x, np.float32).astype(ml_dtypes.bfloat16).astype(np.float64), axis, -1)
    blocks = v.reshape(v.shape[:-1] + (-1, 32))
    amax = np.abs(blocks).max(-1, keepdims=True)
    byte = np.maximum(np.where(amax > 0, np.frexp(amax)[1] - 1 + 127, 0) - down, 1)
    scale = np.exp2(byte - 127.0)
    codes = (blocks / scale).astype(np.float32).astype(dtype).astype(np.float64)
    return np.moveaxis((codes * scale).reshape(v.shape), -1, axis)


WIDE = False


def mx_kscale(k):
    if not WIDE:
        return np.ones(k)
    levels = np.array([10, -10, 5, -5, 0])
    a = np.random.permutation(np.resize(levels, k // 512 * 4)).reshape(k // 512, 4)
    idx = np.arange(k)
    return np.exp2(a[idx // 512, idx % 128 // 32])


BF16 = ml_dtypes.bfloat16


def bf(x):
    return np.asarray(x, np.float32).astype(BF16)


def f64(x):
    return np.asarray(x).astype(np.float64)


E2M1 = np.array([0.0, 0.5, 1.0, 1.5, 2.0, 3.0, 4.0, 6.0, -0.0, -0.5, -1.0, -1.5, -2.0, -3.0, -4.0, -6.0])


def pack_weight(w, fmt):
    k, n = w.shape
    w = f64(bf(w)).reshape(k // 32, 32, n)
    amax = np.abs(w).max(1)
    if fmt == "e4m3":
        byte = np.frexp(amax)[1] - 1 + 127 - 7
    else:
        mant, ex = np.frexp(amax / 6.0)
        byte = np.where(mant > 0.5, ex, ex - 1) + 127
    byte = np.clip(np.where(amax > 0, byte, 1), 1, 254)
    scaled = (w * np.exp2(127.0 - byte)[:, None, :]).reshape(k, n).astype(np.float32)
    by_word = np.ascontiguousarray(scaled.reshape(k // 512, 128, 4, n).transpose(0, 1, 3, 2))
    if fmt == "e4m3":
        words = by_word.astype(ml_dtypes.float8_e4m3fn).view(np.uint8)
    else:
        c = by_word.astype(ml_dtypes.float4_e2m1fn).view(np.uint8) & 0xF
        words = c[..., 0::2] | (c[..., 1::2] << 4)
    return np.ascontiguousarray(words), np.ascontiguousarray(byte.astype(np.uint8).reshape(k // 512, 16, n))


def unpack_weight(words, scales, fmt):
    g, p, n, _ = words.shape
    if fmt == "e4m3":
        vals = np.ascontiguousarray(words).view(ml_dtypes.float8_e4m3fn).astype(np.float64)
    else:
        nib = np.empty((g, p, n, 4), np.uint8)
        nib[..., 0::2] = words & 0xF
        nib[..., 1::2] = words >> 4
        vals = E2M1[nib]
    vals = vals * np.repeat(np.exp2(scales.astype(np.float64) - 127.0), 8, axis=1)[..., None]
    return vals.transpose(0, 1, 3, 2).reshape(g * 512, n)

def pack4(w):
    words, scales = pack_weight(w, "e2m1")
    return words.reshape(words.shape[0], 128, -1), scales


def unpack4(words, scales):
    return unpack_weight(words.reshape(words.shape[0], 128, -1, 2), scales, "e2m1")


B, X_DIM, Z_DIM, K, H = 128, 3584, 64, 512, 512


def elu(v):
    return np.where(v > 0.0, v, np.exp(np.minimum(v, 0.0)) - 1.0)


def softplus(v):
    return np.maximum(v, 0.0) + np.log(1.0 + np.exp(-np.abs(v)))


def setup_inputs():
    s = mx_kscale(H)
    dec_h1 = bf(elu(np.random.standard_normal((B, H))) * s)
    x = bf(np.random.random((B, X_DIM)))
    dw2_words, dw2_scales = pack4(np.random.standard_normal((H, H)) * 1.25 / np.sqrt(H) / s[:, None])
    db2 = bf(np.random.standard_normal(H) * 0.5)
    dw3_words, dw3_scales = pack4(np.random.standard_normal((H, X_DIM)) * 2.5 / np.sqrt(H))
    db3 = bf(np.random.standard_normal(X_DIM) * 0.8)
    return {"dec_h1": dec_h1,
            "x": x,
            "dw2_words": dw2_words,
            "dw2_scales": dw2_scales,
            "db2": db2,
            "dw3_words": dw3_words,
            "dw3_scales": dw3_scales,
            "db3": db3}


def reference(dec_h1, x, dw2_words, dw2_scales, db2, dw3_words, dw3_scales, db3):
    d2 = elu((mxq(f64(dec_h1), 1, "e4m3") @ unpack4(dw2_words, dw2_scales)) + f64(db2))
    logits = (mxq(d2, 1, "e4m3") @ unpack4(dw3_words, dw3_scales)) + f64(db3)
    return np.sum(f64(x) * logits - softplus(logits), axis=-1)

@@ -1,0 +1,170 @@
+from contextlib import ExitStack
+
+import concourse.mybir as mybir
+from concourse.masks import make_identity
+
+F32 = mybir.dt.float32
+BF16 = mybir.dt.bfloat16
+I32 = mybir.dt.int32
+U8 = mybir.dt.uint8
+U32 = mybir.dt.uint32
+FP8X4 = mybir.dt.float8_e4m3fn_x4
+FP4X4 = mybir.dt.float4_e2m1fn_x4
+ALU = mybir.AluOpType
+ACT = mybir.ActivationFunctionType
+
+P = 128
+HIDDEN = 512
+PIXELS = 3584
+BANK = 512
+N_BANKS = PIXELS // BANK
+QUADRANTS = 4
+
+CAP = 30.0
+
+FLOPS = 2 * P * HIDDEN * (HIDDEN + PIXELS)
+
+
+def load_scale_rows(nc, plane, scales):
+    for quadrant in range(QUADRANTS):
+        nc.sync.dma_start(
+            out=plane[32 * quadrant : 32 * quadrant + 4, :].bitcast(I32),
+            in_=scales[4 * quadrant : 4 * quadrant + 4, :].bitcast(I32),
+        )
+
+
+def quantise_rows(nc, psum, keep, ident, rows, name):
+    words = rows.bitcast(F32)
+    turned = psum.tile([P, 2, P], F32, tag="bank", name=name + "_turned")
+    for u in range(2):
+        nc.tensor.transpose(turned[:, u, :], words[:, u : HIDDEN // 2 : 2], ident)
+    grouped = keep.tile([P, 4 * P], BF16, align_bytes=64, name=name + "_grouped")
+    nc.vector.tensor_copy(
+        out=grouped[:].bitcast(F32).rearrange("p (b u) -> p b u", u=2),
+        in_=turned[:].rearrange("p u b -> p b u"),
+    )
+    codes = keep.tile([P, P], U32, align_bytes=64, name=name + "_codes")
+    plane = keep.tile([P, P], U8, align_bytes=64, name=name + "_plane")
+    nc.vector.quantize_mx(out=codes[:].bitcast(FP8X4), scales=plane[:], in_=grouped[:])
+    return codes, plane
+
+
+def tile_gmvae_pb_s_kernel(
+    tc, dec_h1, x, dw2_words, dw2_scales, db2, dw3_words, dw3_scales, db3, out
+):
+    nc = tc.nc
+    with ExitStack() as ctx:
+        keep = ctx.enter_context(tc.tile_pool(name="keep", bufs=1))
+        psum = ctx.enter_context(tc.psum_pool(name="psum", bufs=8))
+
+        w2_plane = keep.tile([P, HIDDEN], U8, align_bytes=64)
+        w3_plane = keep.tile([P, PIXELS], U8, align_bytes=64)
+        nc.vector.memset(w2_plane[:].bitcast(I32), 0)
+        nc.vector.memset(w3_plane[:].bitcast(I32), 0)
+
+        ident = keep.tile([P, P], F32)
+        make_identity(nc, ident[:])
+        ones = keep.tile([P, P], F32)
+        nc.vector.memset(ones[:], 1.0)
+
+        h1 = keep.tile([P, HIDDEN], BF16)
+        nc.sync.dma_start(out=h1[:], in_=dec_h1)
+        load_scale_rows(nc, w2_plane, dw2_scales[0])
+        w2_words = keep.tile([P, 2 * HIDDEN], U8, align_bytes=64)
+        nc.sync.dma_start(out=w2_words[:].bitcast(I32), in_=dw2_words[0].bitcast(I32))
+        b2 = keep.tile([P, HIDDEN], BF16)
+        nc.sync.dma_start(out=b2[:], in_=db2.partition_broadcast(P))
+        load_scale_rows(nc, w3_plane, dw3_scales[0])
+        w3_words = keep.tile([P, 2 * PIXELS], U8, align_bytes=64)
+        nc.sync.dma_start(out=w3_words[:].bitcast(I32), in_=dw3_words[0].bitcast(I32))
+        b3 = keep.tile([P, PIXELS], BF16)
+        nc.sync.dma_start(out=b3[:], in_=db3.partition_broadcast(P))
+        x_sb = keep.tile([P, PIXELS], BF16)
+        nc.sync.dma_start(out=x_sb[:], in_=x)
+
+        h1_codes, h1_plane = quantise_rows(nc, psum, keep, ident[:], h1[:], "h1")
+        z2 = psum.tile([P, HIDDEN], F32, tag="bank")
+        nc.tensor.matmul_mx(
+            out=z2[:],
+            lhsT=h1_codes[:].bitcast(FP8X4),
+            lhsT_scale=h1_plane[:],
+            rhs=w2_words[:].bitcast(FP4X4),
+            rhs_scale=w2_plane[:],
+            start=True,
+            stop=True,
+        )
+        v2 = keep.tile([P, HIDDEN], F32)
+        nc.vector.tensor_tensor(out=v2[:], in0=z2[:], in1=b2[:], op=ALU.add)
+        exp_v2 = keep.tile([P, HIDDEN], F32)
+        nc.scalar.activation(out=exp_v2[:], in_=v2[:], func=ACT.Exp)
+        relu_less_1 = keep.tile([P, HIDDEN], F32)
+        nc.vector.tensor_scalar(
+            out=relu_less_1[:], in0=v2[:], scalar1=0.0, scalar2=-1.0, op0=ALU.max, op1=ALU.add
+        )
+        d2 = keep.tile([P, HIDDEN], BF16)
+        nc.vector.scalar_tensor_tensor(
+            out=d2[:], in0=exp_v2[:], scalar=1.0, in1=relu_less_1[:], op0=ALU.min, op1=ALU.add
+        )
+
+        d2_codes, d2_plane = quantise_rows(nc, psum, keep, ident[:], d2[:], "d2")
+        logits = keep.tile([P, PIXELS], F32)
+        capped = keep.tile([P, PIXELS], F32)
+        grown = keep.tile([P, PIXELS], F32)
+        plus = keep.tile([P, N_BANKS + 1], F32)
+        for i in range(N_BANKS):
+            cols = slice(i * BANK, (i + 1) * BANK)
+            z3 = psum.tile([P, BANK], F32, tag="bank", name="z3_%d" % i)
+            nc.tensor.matmul_mx(
+                out=z3[:],
+                lhsT=d2_codes[:].bitcast(FP8X4),
+                lhsT_scale=d2_plane[:],
+                rhs=w3_words[:, 2 * i * BANK : 2 * (i + 1) * BANK].bitcast(FP4X4),
+                rhs_scale=w3_plane[:, cols],
+                start=True,
+                stop=True,
+            )
+            nc.vector.tensor_tensor(out=logits[:, cols], in0=z3[:], in1=b3[:, cols], op=ALU.add)
+            nc.vector.tensor_scalar(
+                out=capped[:, cols],
+                in0=logits[:, cols],
+                scalar1=CAP,
+                scalar2=None,
+                op0=ALU.min,
+                op1=ALU.add,
+                accum_out=plus[:, i : i + 1],
+            )
+            nc.scalar.activation(out=grown[:, cols], in_=capped[:, cols], func=ACT.Exp)
+
+        log_sum = keep.tile([P, 1], F32)
+        nc.scalar.activation(
+            out=grown[:], in_=grown[:], func=ACT.Ln, bias=1.0, accum_out=log_sum[:]
+        )
+        product = keep.tile([P, PIXELS], F32)
+        nc.vector.scalar_tensor_tensor(
+            out=product[:],
+            in0=x_sb[:],
+            scalar=1.0,
+            in1=logits[:],
+            op0=ALU.subtract,
+            op1=ALU.mult,
+            accum_out=plus[:, N_BANKS : N_BANKS + 1],
+        )
+        plus_sum = keep.tile([P, 1], F32)
+        nc.vector.tensor_reduce(
+            out=plus_sum[:], in_=plus[:], axis=mybir.AxisListType.X, op=ALU.add
+        )
+
+        repeated = keep.tile([P, P], F32)
+        nc.vector.tensor_scalar(
+            out=repeated[:],
+            in0=ones[:],
+            scalar1=plus_sum[:, 0:1],
+            scalar2=log_sum[:, 0:1],
+            op0=ALU.mult,
+            op1=ALU.subtract,
+        )
+        as_rows = psum.tile([P, P], F32, tag="bank")
+        nc.tensor.transpose(as_rows[:], repeated[:], ident[:])
+        result = keep.tile([P, P], F32)
+        nc.vector.tensor_copy(out=result[:], in_=as_rows[:])
+        nc.sync.dma_start(out=out.rearrange("(o b) -> o b", o=1), in_=result[0:1, :])

@@ -78,7 +78,9 @@ def tile_gmvae_pb_s_kernel(
         w3_words = keep.tile([P, 2 * PIXELS], U8, align_bytes=64)
         nc.sync.dma_start(out=w3_words[:].bitcast(I32), in_=dw3_words[0].bitcast(I32))
         b3 = keep.tile([P, PIXELS], BF16)
-        nc.sync.dma_start(out=b3[:], in_=db3.partition_broadcast(P))
+        for i in range(N_BANKS):
+            cols = slice(i * BANK, (i + 1) * BANK)
+            nc.sync.dma_start(out=b3[:, cols], in_=db3[cols].partition_broadcast(P))
         x_sb = keep.tile([P, PIXELS], BF16)
         nc.sync.dma_start(out=x_sb[:], in_=x)
 

@@ -20,8 +20,6 @@ BANK = 512
 N_BANKS = PIXELS // BANK
 QUADRANTS = 4
 
-CAP = 30.0
-
 FLOPS = 2 * P * HIDDEN * (HIDDEN + PIXELS)
 
 
@@ -54,6 +52,7 @@ def tile_gmvae_pb_s_kernel(
 ):
     nc = tc.nc
     with ExitStack() as ctx:
+        ctx.enter_context(tc.manual_schedule())
         keep = ctx.enter_context(tc.tile_pool(name="keep", bufs=1))
         psum = ctx.enter_context(tc.psum_pool(name="psum", bufs=8))
 
@@ -78,9 +77,7 @@ def tile_gmvae_pb_s_kernel(
         w3_words = keep.tile([P, 2 * PIXELS], U8, align_bytes=64)
         nc.sync.dma_start(out=w3_words[:].bitcast(I32), in_=dw3_words[0].bitcast(I32))
         b3 = keep.tile([P, PIXELS], BF16)
-        for i in range(N_BANKS):
-            cols = slice(i * BANK, (i + 1) * BANK)
-            nc.sync.dma_start(out=b3[:, cols], in_=db3[cols].partition_broadcast(P))
+        nc.sync.dma_start(out=b3[:], in_=db3.partition_broadcast(P))
         x_sb = keep.tile([P, PIXELS], BF16)
         nc.sync.dma_start(out=x_sb[:], in_=x)
 
@@ -109,58 +106,111 @@ def tile_gmvae_pb_s_kernel(
         )
 
         d2_codes, d2_plane = quantise_rows(nc, psum, keep, ident[:], d2[:], "d2")
-        logits = keep.tile([P, PIXELS], F32)
-        capped = keep.tile([P, PIXELS], F32)
-        grown = keep.tile([P, PIXELS], F32)
-        plus = keep.tile([P, N_BANKS + 1], F32)
+        z3 = []
         for i in range(N_BANKS):
-            cols = slice(i * BANK, (i + 1) * BANK)
-            z3 = psum.tile([P, BANK], F32, tag="bank", name="z3_%d" % i)
+            z3.append(psum.tile([P, BANK], F32, tag="bank", name="z3_%d" % i))
             nc.tensor.matmul_mx(
-                out=z3[:],
+                out=z3[i][:],
                 lhsT=d2_codes[:].bitcast(FP8X4),
                 lhsT_scale=d2_plane[:],
                 rhs=w3_words[:, 2 * i * BANK : 2 * (i + 1) * BANK].bitcast(FP4X4),
-                rhs_scale=w3_plane[:, cols],
+                rhs_scale=w3_plane[:, i * BANK : (i + 1) * BANK],
                 start=True,
                 stop=True,
             )
-            nc.vector.tensor_tensor(out=logits[:, cols], in0=z3[:], in1=b3[:, cols], op=ALU.add)
-            nc.vector.tensor_scalar(
-                out=capped[:, cols],
-                in0=logits[:, cols],
-                scalar1=CAP,
-                scalar2=None,
-                op0=ALU.min,
-                op1=ALU.add,
-                accum_out=plus[:, i : i + 1],
+
+        logits = keep.tile([P, PIXELS], F32)
+        size = keep.tile([P, PIXELS], F32)
+        decay = keep.tile([P, PIXELS], F32)
+        size_sums_scalar = keep.tile([P, (N_BANKS + 1) // 2], F32)
+        size_sums_vector = keep.tile([P, N_BANKS // 2], F32)
+
+        def bank(i):
+            return slice(i * BANK, (i + 1) * BANK)
+
+        def add_bias(i):
+            nc.vector.tensor_tensor(
+                out=logits[:, bank(i)], in0=z3[i][:], in1=b3[:, bank(i)], op=ALU.add
             )
-            nc.scalar.activation(out=grown[:, cols], in_=capped[:, cols], func=ACT.Exp)
+
+        def size_on_scalar(i):
+            nc.scalar.activation(
+                out=size[:, bank(i)],
+                in_=logits[:, bank(i)],
+                func=ACT.Abs,
+                accum_out=size_sums_scalar[:, i // 2 : i // 2 + 1],
+            )
+
+        def size_on_vector(i):
+            nc.vector.scalar_tensor_tensor(
+                out=size[:, bank(i)],
+                in0=logits[:, bank(i)],
+                scalar=-1.0,
+                in1=logits[:, bank(i)],
+                op0=ALU.mult,
+                op1=ALU.max,
+                accum_out=size_sums_vector[:, i // 2 : i // 2 + 1],
+            )
+
+        def exponential(i):
+            nc.scalar.activation(
+                out=decay[:, bank(i)], in_=size[:, bank(i)], func=ACT.Exp, scale=-1.0
+            )
+
+        for even in range(0, N_BANKS, 2):
+            odd_before = even - 1
+            for i in (even, even + 1):
+                if i < N_BANKS:
+                    add_bias(i)
+            if odd_before > 0:
+                size_on_vector(odd_before)
+            size_on_scalar(even)
+            exponential(even)
+            if odd_before > 0:
+                exponential(odd_before)
 
         log_sum = keep.tile([P, 1], F32)
         nc.scalar.activation(
-            out=grown[:], in_=grown[:], func=ACT.Ln, bias=1.0, accum_out=log_sum[:]
+            out=decay[:], in_=decay[:], func=ACT.Ln, bias=1.0, accum_out=log_sum[:]
         )
         product = keep.tile([P, PIXELS], F32)
+        product_sum = keep.tile([P, 1], F32)
         nc.vector.scalar_tensor_tensor(
             out=product[:],
             in0=x_sb[:],
-            scalar=1.0,
+            scalar=0.5,
             in1=logits[:],
             op0=ALU.subtract,
             op1=ALU.mult,
-            accum_out=plus[:, N_BANKS : N_BANKS + 1],
+            accum_out=product_sum[:],
         )
-        plus_sum = keep.tile([P, 1], F32)
+        size_sum_scalar = keep.tile([P, 1], F32)
         nc.vector.tensor_reduce(
-            out=plus_sum[:], in_=plus[:], axis=mybir.AxisListType.X, op=ALU.add
+            out=size_sum_scalar[:], in_=size_sums_scalar[:], axis=mybir.AxisListType.X, op=ALU.add
+        )
+        size_sum_vector = keep.tile([P, 1], F32)
+        nc.vector.tensor_reduce(
+            out=size_sum_vector[:], in_=size_sums_vector[:], axis=mybir.AxisListType.X, op=ALU.add
+        )
+        size_sum = keep.tile([P, 1], F32)
+        nc.vector.tensor_tensor(
+            out=size_sum[:], in0=size_sum_scalar[:], in1=size_sum_vector[:], op=ALU.add
+        )
+        without_log = keep.tile([P, 1], F32)
+        nc.vector.scalar_tensor_tensor(
+            out=without_log[:],
+            in0=size_sum[:],
+            scalar=-0.5,
+            in1=product_sum[:],
+            op0=ALU.mult,
+            op1=ALU.add,
         )
 
         repeated = keep.tile([P, P], F32)
         nc.vector.tensor_scalar(
             out=repeated[:],
             in0=ones[:],
-            scalar1=plus_sum[:, 0:1],
+            scalar1=without_log[:, 0:1],
             scalar2=log_sum[:, 0:1],
             op0=ALU.mult,
             op1=ALU.subtract,

@@ -66,13 +66,14 @@ def tile_gmvae_pb_s_kernel(
         ones = keep.tile([P, P], F32)
         nc.vector.memset(ones[:], 1.0)
 
+        b2 = keep.tile([P, HIDDEN], BF16)
+        nc.scalar.dma_start(out=b2[:], in_=db2.partition_broadcast(P))
+
         h1 = keep.tile([P, HIDDEN], BF16)
         nc.sync.dma_start(out=h1[:], in_=dec_h1)
         load_scale_rows(nc, w2_plane, dw2_scales[0])
         w2_words = keep.tile([P, 2 * HIDDEN], U8, align_bytes=64)
         nc.sync.dma_start(out=w2_words[:].bitcast(I32), in_=dw2_words[0].bitcast(I32))
-        b2 = keep.tile([P, HIDDEN], BF16)
-        nc.sync.dma_start(out=b2[:], in_=db2.partition_broadcast(P))
         load_scale_rows(nc, w3_plane, dw3_scales[0])
         w3_words = keep.tile([P, 2 * PIXELS], U8, align_bytes=64)
         nc.sync.dma_start(out=w3_words[:].bitcast(I32), in_=dw3_words[0].bitcast(I32))

@@ -37,7 +37,7 @@ def quantise_rows(nc, psum, keep, ident, rows, name):
     for u in range(2):
         nc.tensor.transpose(turned[:, u, :], words[:, u : HIDDEN // 2 : 2], ident)
     grouped = keep.tile([P, 4 * P], BF16, align_bytes=64, name=name + "_grouped")
-    nc.vector.tensor_copy(
+    nc.scalar.copy(
         out=grouped[:].bitcast(F32).rearrange("p (b u) -> p b u", u=2),
         in_=turned[:].rearrange("p u b -> p b u"),
     )
@@ -56,6 +56,8 @@ def tile_gmvae_pb_s_kernel(
         keep = ctx.enter_context(tc.tile_pool(name="keep", bufs=1))
         psum = ctx.enter_context(tc.psum_pool(name="psum", bufs=8))
 
+        b2_row = keep.tile([P, HIDDEN], BF16)
+        nc.vector.memset(b2_row[:], 0.0)
         w2_plane = keep.tile([P, HIDDEN], U8, align_bytes=64)
         w3_plane = keep.tile([P, PIXELS], U8, align_bytes=64)
         nc.vector.memset(w2_plane[:].bitcast(I32), 0)
@@ -65,12 +67,12 @@ def tile_gmvae_pb_s_kernel(
         make_identity(nc, ident[:])
         ones = keep.tile([P, P], F32)
         nc.vector.memset(ones[:], 1.0)
-
-        b2 = keep.tile([P, HIDDEN], BF16)
-        nc.scalar.dma_start(out=b2[:], in_=db2.partition_broadcast(P))
+        ones_bf16 = keep.tile([P, P], BF16)
+        nc.vector.memset(ones_bf16[:], 1.0)
 
         h1 = keep.tile([P, HIDDEN], BF16)
         nc.sync.dma_start(out=h1[:], in_=dec_h1)
+        nc.sync.dma_start(out=b2_row[0:1, :], in_=db2.rearrange("(o h) -> o h", o=1))
         load_scale_rows(nc, w2_plane, dw2_scales[0])
         w2_words = keep.tile([P, 2 * HIDDEN], U8, align_bytes=64)
         nc.sync.dma_start(out=w2_words[:].bitcast(I32), in_=dw2_words[0].bitcast(I32))
@@ -83,6 +85,10 @@ def tile_gmvae_pb_s_kernel(
         nc.sync.dma_start(out=x_sb[:], in_=x)
 
         h1_codes, h1_plane = quantise_rows(nc, psum, keep, ident[:], h1[:], "h1")
+        b2_spread = psum.tile([P, HIDDEN], F32, tag="bank")
+        nc.tensor.matmul(out=b2_spread[:], lhsT=ones_bf16[:], rhs=b2_row[:], start=True, stop=True)
+        b2 = keep.tile([P, HIDDEN], F32)
+        nc.scalar.copy(out=b2[:], in_=b2_spread[:])
         z2 = psum.tile([P, HIDDEN], F32, tag="bank")
         nc.tensor.matmul_mx(
             out=z2[:],
@@ -94,17 +100,31 @@ def tile_gmvae_pb_s_kernel(
             stop=True,
         )
         v2 = keep.tile([P, HIDDEN], F32)
-        nc.vector.tensor_tensor(out=v2[:], in0=z2[:], in1=b2[:], op=ALU.add)
         exp_v2 = keep.tile([P, HIDDEN], F32)
-        nc.scalar.activation(out=exp_v2[:], in_=v2[:], func=ACT.Exp)
         relu_less_1 = keep.tile([P, HIDDEN], F32)
-        nc.vector.tensor_scalar(
-            out=relu_less_1[:], in0=v2[:], scalar1=0.0, scalar2=-1.0, op0=ALU.max, op1=ALU.add
-        )
         d2 = keep.tile([P, HIDDEN], BF16)
-        nc.vector.scalar_tensor_tensor(
-            out=d2[:], in0=exp_v2[:], scalar=1.0, in1=relu_less_1[:], op0=ALU.min, op1=ALU.add
-        )
+        halves = (slice(0, HIDDEN // 2), slice(HIDDEN // 2, HIDDEN))
+        for cols in halves:
+            nc.vector.tensor_tensor(out=v2[:, cols], in0=z2[:, cols], in1=b2[:, cols], op=ALU.add)
+            nc.scalar.activation(out=exp_v2[:, cols], in_=v2[:, cols], func=ACT.Exp)
+        for cols in halves:
+            nc.vector.tensor_scalar(
+                out=relu_less_1[:, cols],
+                in0=v2[:, cols],
+                scalar1=0.0,
+                scalar2=-1.0,
+                op0=ALU.max,
+                op1=ALU.add,
+            )
+        for cols in halves:
+            nc.vector.scalar_tensor_tensor(
+                out=d2[:, cols],
+                in0=exp_v2[:, cols],
+                scalar=1.0,
+                in1=relu_less_1[:, cols],
+                op0=ALU.min,
+                op1=ALU.add,
+            )
 
         d2_codes, d2_plane = quantise_rows(nc, psum, keep, ident[:], d2[:], "d2")
         z3 = []

@@ -80,7 +80,9 @@ def tile_gmvae_pb_s_kernel(
         w3_words = keep.tile([P, 2 * PIXELS], U8, align_bytes=64)
         nc.sync.dma_start(out=w3_words[:].bitcast(I32), in_=dw3_words[0].bitcast(I32))
         b3 = keep.tile([P, PIXELS], BF16)
-        nc.sync.dma_start(out=b3[:], in_=db3.partition_broadcast(P))
+        for i in range(N_BANKS):
+            cols = slice(i * BANK, (i + 1) * BANK)
+            nc.sync.dma_start(out=b3[:, cols], in_=db3[cols].partition_broadcast(P))
         x_sb = keep.tile([P, PIXELS], BF16)
         nc.sync.dma_start(out=x_sb[:], in_=x)
 

@@ -18,31 +18,39 @@ HIDDEN = 512
 PIXELS = 3584
 BANK = 512
 N_BANKS = PIXELS // BANK
+assert N_BANKS % 2 == 1
+PACK = 4
+PAIRS = PACK // 2
 QUADRANTS = 4
+QUADRANT = P // QUADRANTS
+LIVE_ROWS = 4
+FP4_WORD_BYTES = 2
+MX_ALIGN = 64
 
 FLOPS = 2 * P * HIDDEN * (HIDDEN + PIXELS)
 
 
 def load_scale_rows(nc, plane, scales):
     for quadrant in range(QUADRANTS):
+        first = QUADRANT * quadrant
         nc.sync.dma_start(
-            out=plane[32 * quadrant : 32 * quadrant + 4, :].bitcast(I32),
-            in_=scales[4 * quadrant : 4 * quadrant + 4, :].bitcast(I32),
+            out=plane[first : first + LIVE_ROWS, :].bitcast(I32),
+            in_=scales[LIVE_ROWS * quadrant : LIVE_ROWS * (quadrant + 1), :].bitcast(I32),
         )
 
 
 def quantise_rows(nc, psum, keep, ident, rows, name):
     words = rows.bitcast(F32)
-    turned = psum.tile([P, 2, P], F32, tag="bank", name=name + "_turned")
-    for u in range(2):
-        nc.tensor.transpose(turned[:, u, :], words[:, u : HIDDEN // 2 : 2], ident)
-    grouped = keep.tile([P, 4 * P], BF16, align_bytes=64, name=name + "_grouped")
+    turned = psum.tile([P, PAIRS, P], F32, tag="bank", name=name + "_turned")
+    for u in range(PAIRS):
+        nc.tensor.transpose(turned[:, u, :], words[:, u : HIDDEN // 2 : PAIRS], ident)
+    grouped = keep.tile([P, PACK * P], BF16, align_bytes=MX_ALIGN, name=name + "_grouped")
     nc.scalar.copy(
-        out=grouped[:].bitcast(F32).rearrange("p (b u) -> p b u", u=2),
+        out=grouped[:].bitcast(F32).rearrange("p (b u) -> p b u", u=PAIRS),
         in_=turned[:].rearrange("p u b -> p b u"),
     )
-    codes = keep.tile([P, P], U32, align_bytes=64, name=name + "_codes")
-    plane = keep.tile([P, P], U8, align_bytes=64, name=name + "_plane")
+    codes = keep.tile([P, P], U32, align_bytes=MX_ALIGN, name=name + "_codes")
+    plane = keep.tile([P, P], U8, align_bytes=MX_ALIGN, name=name + "_plane")
     nc.vector.quantize_mx(out=codes[:].bitcast(FP8X4), scales=plane[:], in_=grouped[:])
     return codes, plane
 
@@ -58,8 +66,8 @@ def tile_gmvae_pb_s_kernel(
 
         b2_row = keep.tile([P, HIDDEN], BF16)
         nc.vector.memset(b2_row[:], 0.0)
-        w2_plane = keep.tile([P, HIDDEN], U8, align_bytes=64)
-        w3_plane = keep.tile([P, PIXELS], U8, align_bytes=64)
+        w2_plane = keep.tile([P, HIDDEN], U8, align_bytes=MX_ALIGN)
+        w3_plane = keep.tile([P, PIXELS], U8, align_bytes=MX_ALIGN)
         nc.vector.memset(w2_plane[:].bitcast(I32), 0)
         nc.vector.memset(w3_plane[:].bitcast(I32), 0)
 
@@ -74,15 +82,13 @@ def tile_gmvae_pb_s_kernel(
         nc.sync.dma_start(out=h1[:], in_=dec_h1)
         nc.sync.dma_start(out=b2_row[0:1, :], in_=db2.rearrange("(o h) -> o h", o=1))
         load_scale_rows(nc, w2_plane, dw2_scales[0])
-        w2_words = keep.tile([P, 2 * HIDDEN], U8, align_bytes=64)
+        w2_words = keep.tile([P, FP4_WORD_BYTES * HIDDEN], U8, align_bytes=MX_ALIGN)
         nc.sync.dma_start(out=w2_words[:].bitcast(I32), in_=dw2_words[0].bitcast(I32))
         load_scale_rows(nc, w3_plane, dw3_scales[0])
-        w3_words = keep.tile([P, 2 * PIXELS], U8, align_bytes=64)
+        w3_words = keep.tile([P, FP4_WORD_BYTES * PIXELS], U8, align_bytes=MX_ALIGN)
         nc.sync.dma_start(out=w3_words[:].bitcast(I32), in_=dw3_words[0].bitcast(I32))
         b3 = keep.tile([P, PIXELS], BF16)
-        for i in range(N_BANKS):
-            cols = slice(i * BANK, (i + 1) * BANK)
-            nc.sync.dma_start(out=b3[:, cols], in_=db3[cols].partition_broadcast(P))
+        nc.sync.dma_start(out=b3[:], in_=db3.partition_broadcast(P))
         x_sb = keep.tile([P, PIXELS], BF16)
         nc.sync.dma_start(out=x_sb[:], in_=x)
 
@@ -136,7 +142,9 @@ def tile_gmvae_pb_s_kernel(
                 out=z3[i][:],
                 lhsT=d2_codes[:].bitcast(FP8X4),
                 lhsT_scale=d2_plane[:],
-                rhs=w3_words[:, 2 * i * BANK : 2 * (i + 1) * BANK].bitcast(FP4X4),
+                rhs=w3_words[
+                    :, FP4_WORD_BYTES * i * BANK : FP4_WORD_BYTES * (i + 1) * BANK
+                ].bitcast(FP4X4),
                 rhs_scale=w3_plane[:, i * BANK : (i + 1) * BANK],
                 start=True,
                 stop=True,
@@ -180,17 +188,17 @@ def tile_gmvae_pb_s_kernel(
                 out=decay[:, bank(i)], in_=size[:, bank(i)], func=ACT.Exp, scale=-1.0
             )
 
-        for even in range(0, N_BANKS, 2):
-            odd_before = even - 1
-            for i in (even, even + 1):
-                if i < N_BANKS:
-                    add_bias(i)
-            if odd_before > 0:
-                size_on_vector(odd_before)
+        add_bias(0)
+        size_on_scalar(0)
+        exponential(0)
+        for odd in range(1, N_BANKS, 2):
+            even = odd + 1
+            add_bias(odd)
+            add_bias(even)
+            size_on_vector(odd)
             size_on_scalar(even)
+            exponential(odd)
             exponential(even)
-            if odd_before > 0:
-                exponential(odd_before)
 
         log_sum = keep.tile([P, 1], F32)
         nc.scalar.activation(

@@ -24,6 +24,8 @@ PAIRS = PACK // 2
 QUADRANTS = 4
 QUADRANT = P // QUADRANTS
 LIVE_ROWS = 4
+SOFTPLUS_CAP = 32.0
+ABS_BANKS = 2
 FP4_WORD_BYTES = 2
 MX_ALIGN = 64
 
@@ -151,10 +153,9 @@ def tile_gmvae_pb_s_kernel(
             )
 
         logits = keep.tile([P, PIXELS], F32)
-        size = keep.tile([P, PIXELS], F32)
-        decay = keep.tile([P, PIXELS], F32)
-        size_sums_scalar = keep.tile([P, (N_BANKS + 1) // 2], F32)
-        size_sums_vector = keep.tile([P, N_BANKS // 2], F32)
+        clipped = keep.tile([P, PIXELS], F32)
+        growth = keep.tile([P, PIXELS], F32)
+        size_sums = keep.tile([P, ABS_BANKS], F32)
 
         def bank(i):
             return slice(i * BANK, (i + 1) * BANK)
@@ -164,68 +165,81 @@ def tile_gmvae_pb_s_kernel(
                 out=logits[:, bank(i)], in0=z3[i][:], in1=b3[:, bank(i)], op=ALU.add
             )
 
-        def size_on_scalar(i):
+        def exp_of_size(i):
             nc.scalar.activation(
-                out=size[:, bank(i)],
+                out=clipped[:, bank(i)],
                 in_=logits[:, bank(i)],
                 func=ACT.Abs,
-                accum_out=size_sums_scalar[:, i // 2 : i // 2 + 1],
+                accum_out=size_sums[:, i : i + 1],
             )
-
-        def size_on_vector(i):
-            nc.vector.scalar_tensor_tensor(
-                out=size[:, bank(i)],
-                in0=logits[:, bank(i)],
-                scalar=-1.0,
-                in1=logits[:, bank(i)],
-                op0=ALU.mult,
-                op1=ALU.max,
-                accum_out=size_sums_vector[:, i // 2 : i // 2 + 1],
-            )
-
-        def exponential(i):
             nc.scalar.activation(
-                out=decay[:, bank(i)], in_=size[:, bank(i)], func=ACT.Exp, scale=-1.0
+                out=growth[:, bank(i)], in_=clipped[:, bank(i)], func=ACT.Exp, scale=-1.0
             )
+
+        def exp_of_cap(i):
+            nc.vector.tensor_scalar(
+                out=clipped[:, bank(i)],
+                in0=logits[:, bank(i)],
+                scalar1=SOFTPLUS_CAP,
+                scalar2=None,
+                op0=ALU.min,
+            )
+            nc.scalar.activation(out=growth[:, bank(i)], in_=clipped[:, bank(i)], func=ACT.Exp)
 
         add_bias(0)
-        size_on_scalar(0)
-        exponential(0)
-        for odd in range(1, N_BANKS, 2):
-            even = odd + 1
-            add_bias(odd)
-            add_bias(even)
-            size_on_vector(odd)
-            size_on_scalar(even)
-            exponential(odd)
-            exponential(even)
+        for i in range(N_BANKS):
+            if i + 1 < N_BANKS:
+                add_bias(i + 1)
+            if i < ABS_BANKS:
+                exp_of_size(i)
+            else:
+                exp_of_cap(i)
+
+        w_turned = psum.tile([P, P], F32, tag="bank")
+        first_block, blocks = ABS_BANKS * BANK // P, PIXELS // P
+        for n in range(first_block, blocks):
+            nc.tensor.matmul(
+                out=w_turned[:],
+                lhsT=clipped[:, n * P : (n + 1) * P],
+                rhs=ident[:],
+                is_transpose=True,
+                start=(n == first_block),
+                stop=(n == blocks - 1),
+            )
 
         log_sum = keep.tile([P, 1], F32)
         nc.scalar.activation(
-            out=decay[:], in_=decay[:], func=ACT.Ln, bias=1.0, accum_out=log_sum[:]
+            out=growth[:], in_=growth[:], func=ACT.Ln, bias=1.0, accum_out=log_sum[:]
         )
         product = keep.tile([P, PIXELS], F32)
+        product_sums = keep.tile([P, 2], F32)
+
+        def weigh(first, last, middle, j):
+            nc.vector.scalar_tensor_tensor(
+                out=product[:, first:last],
+                in0=x_sb[:, first:last],
+                scalar=middle,
+                in1=logits[:, first:last],
+                op0=ALU.subtract,
+                op1=ALU.mult,
+                accum_out=product_sums[:, j : j + 1],
+            )
+
+        weigh(0, ABS_BANKS * BANK, 0.5, 0)
+        w_blocks = keep.tile([P, P], F32)
+        nc.vector.tensor_copy(out=w_blocks[:], in_=w_turned[:])
+        w_row = psum.tile([P, P], F32, tag="bank")
+        nc.tensor.matmul(out=w_row[:], lhsT=ones[:], rhs=w_blocks[:], start=True, stop=True)
+        weigh(ABS_BANKS * BANK, PIXELS, 1.0, 1)
+        w_sum = keep.tile([P, P], F32)
+        nc.vector.tensor_copy(out=w_sum[:], in_=w_row[:])
         product_sum = keep.tile([P, 1], F32)
-        nc.vector.scalar_tensor_tensor(
-            out=product[:],
-            in0=x_sb[:],
-            scalar=0.5,
-            in1=logits[:],
-            op0=ALU.subtract,
-            op1=ALU.mult,
-            accum_out=product_sum[:],
-        )
-        size_sum_scalar = keep.tile([P, 1], F32)
-        nc.vector.tensor_reduce(
-            out=size_sum_scalar[:], in_=size_sums_scalar[:], axis=mybir.AxisListType.X, op=ALU.add
-        )
-        size_sum_vector = keep.tile([P, 1], F32)
-        nc.vector.tensor_reduce(
-            out=size_sum_vector[:], in_=size_sums_vector[:], axis=mybir.AxisListType.X, op=ALU.add
+        nc.vector.tensor_tensor(
+            out=product_sum[:], in0=product_sums[:, 0:1], in1=product_sums[:, 1:2], op=ALU.add
         )
         size_sum = keep.tile([P, 1], F32)
-        nc.vector.tensor_tensor(
-            out=size_sum[:], in0=size_sum_scalar[:], in1=size_sum_vector[:], op=ALU.add
+        nc.vector.tensor_reduce(
+            out=size_sum[:], in_=size_sums[:], axis=mybir.AxisListType.X, op=ALU.add
         )
         without_log = keep.tile([P, 1], F32)
         nc.vector.scalar_tensor_tensor(
@@ -249,5 +263,5 @@ def tile_gmvae_pb_s_kernel(
         as_rows = psum.tile([P, P], F32, tag="bank")
         nc.tensor.transpose(as_rows[:], repeated[:], ident[:])
         result = keep.tile([P, P], F32)
-        nc.vector.tensor_copy(out=result[:], in_=as_rows[:])
+        nc.vector.tensor_tensor(out=result[:], in0=as_rows[:], in1=w_sum[:], op=ALU.add)
         nc.sync.dma_start(out=out.rearrange("(o b) -> o b", o=1), in_=result[0:1, :])

@@ -24,7 +24,9 @@ PAIRS = PACK // 2
 QUADRANTS = 4
 QUADRANT = P // QUADRANTS
 LIVE_ROWS = 4
-SOFTPLUS_CAP = 32.0
+SOFTPLUS_CAP = 20.0
+EARLY_BANKS = 2
+N_PAIRS = 2
 ABS_BANKS = 2
 FP4_WORD_BYTES = 2
 MX_ALIGN = 64
@@ -88,9 +90,16 @@ def tile_gmvae_pb_s_kernel(
         nc.sync.dma_start(out=w2_words[:].bitcast(I32), in_=dw2_words[0].bitcast(I32))
         load_scale_rows(nc, w3_plane, dw3_scales[0])
         w3_words = keep.tile([P, FP4_WORD_BYTES * PIXELS], U8, align_bytes=MX_ALIGN)
-        nc.sync.dma_start(out=w3_words[:].bitcast(I32), in_=dw3_words[0].bitcast(I32))
+        w3_early = slice(0, FP4_WORD_BYTES * EARLY_BANKS * BANK)
+        w3_late = slice(FP4_WORD_BYTES * EARLY_BANKS * BANK, FP4_WORD_BYTES * PIXELS)
+        nc.sync.dma_start(
+            out=w3_words[:, w3_early].bitcast(I32), in_=dw3_words[0][:, w3_early].bitcast(I32)
+        )
         b3 = keep.tile([P, PIXELS], BF16)
         nc.sync.dma_start(out=b3[:], in_=db3.partition_broadcast(P))
+        nc.sync.dma_start(
+            out=w3_words[:, w3_late].bitcast(I32), in_=dw3_words[0][:, w3_late].bitcast(I32)
+        )
         x_sb = keep.tile([P, PIXELS], BF16)
         nc.sync.dma_start(out=x_sb[:], in_=x)
 
@@ -152,7 +161,7 @@ def tile_gmvae_pb_s_kernel(
                 stop=True,
             )
 
-        logits = keep.tile([P, PIXELS], F32)
+        minus_v = keep.tile([P, PIXELS], F32)
         clipped = keep.tile([P, PIXELS], F32)
         growth = keep.tile([P, PIXELS], F32)
         size_sums = keep.tile([P, ABS_BANKS], F32)
@@ -161,30 +170,38 @@ def tile_gmvae_pb_s_kernel(
             return slice(i * BANK, (i + 1) * BANK)
 
         def add_bias(i):
-            nc.vector.tensor_tensor(
-                out=logits[:, bank(i)], in0=z3[i][:], in1=b3[:, bank(i)], op=ALU.add
+            nc.vector.scalar_tensor_tensor(
+                out=minus_v[:, bank(i)],
+                in0=z3[i][:],
+                scalar=-1.0,
+                in1=b3[:, bank(i)],
+                op0=ALU.mult,
+                op1=ALU.subtract,
             )
 
         def exp_of_size(i):
             nc.scalar.activation(
                 out=clipped[:, bank(i)],
-                in_=logits[:, bank(i)],
+                in_=minus_v[:, bank(i)],
                 func=ACT.Abs,
+                scale=0.5,
                 accum_out=size_sums[:, i : i + 1],
             )
             nc.scalar.activation(
-                out=growth[:, bank(i)], in_=clipped[:, bank(i)], func=ACT.Exp, scale=-1.0
+                out=growth[:, bank(i)], in_=clipped[:, bank(i)], func=ACT.Exp, scale=-2.0
             )
 
         def exp_of_cap(i):
             nc.vector.tensor_scalar(
                 out=clipped[:, bank(i)],
-                in0=logits[:, bank(i)],
-                scalar1=SOFTPLUS_CAP,
+                in0=minus_v[:, bank(i)],
+                scalar1=-SOFTPLUS_CAP,
                 scalar2=None,
-                op0=ALU.min,
+                op0=ALU.max,
             )
-            nc.scalar.activation(out=growth[:, bank(i)], in_=clipped[:, bank(i)], func=ACT.Exp)
+            nc.scalar.activation(
+                out=growth[:, bank(i)], in_=clipped[:, bank(i)], func=ACT.Exp, scale=-1.0
+            )
 
         add_bias(0)
         for i in range(N_BANKS):
@@ -207,9 +224,37 @@ def tile_gmvae_pb_s_kernel(
                 stop=(n == blocks - 1),
             )
 
-        log_sum = keep.tile([P, 1], F32)
+        pair_products = keep.tile([P, N_PAIRS * BANK], F32)
+        plus_one = keep.tile([P, N_PAIRS * BANK], F32)
+        for j in range(N_PAIRS):
+            nc.vector.tensor_scalar(
+                out=plus_one[:, bank(j)],
+                in0=growth[:, bank(2 * j)],
+                scalar1=1.0,
+                scalar2=None,
+                op0=ALU.add,
+            )
+        for j in range(N_PAIRS):
+            nc.vector.scalar_tensor_tensor(
+                out=pair_products[:, bank(j)],
+                in0=growth[:, bank(2 * j + 1)],
+                scalar=1.0,
+                in1=plus_one[:, bank(j)],
+                op0=ALU.add,
+                op1=ALU.mult,
+            )
+
+        log_sums = keep.tile([P, 2], F32)
+        single = slice(2 * N_PAIRS * BANK, PIXELS)
         nc.scalar.activation(
-            out=growth[:], in_=growth[:], func=ACT.Ln, bias=1.0, accum_out=log_sum[:]
+            out=growth[:, single],
+            in_=growth[:, single],
+            func=ACT.Ln,
+            bias=1.0,
+            accum_out=log_sums[:, 0:1],
+        )
+        nc.scalar.activation(
+            out=pair_products[:], in_=pair_products[:], func=ACT.Ln, accum_out=log_sums[:, 1:2]
         )
         product = keep.tile([P, PIXELS], F32)
         product_sums = keep.tile([P, 2], F32)
@@ -219,7 +264,7 @@ def tile_gmvae_pb_s_kernel(
                 out=product[:, first:last],
                 in0=x_sb[:, first:last],
                 scalar=middle,
-                in1=logits[:, first:last],
+                in1=minus_v[:, first:last],
                 op0=ALU.subtract,
                 op1=ALU.mult,
                 accum_out=product_sums[:, j : j + 1],
@@ -228,40 +273,23 @@ def tile_gmvae_pb_s_kernel(
         weigh(0, ABS_BANKS * BANK, 0.5, 0)
         w_blocks = keep.tile([P, P], F32)
         nc.vector.tensor_copy(out=w_blocks[:], in_=w_turned[:])
-        w_row = psum.tile([P, P], F32, tag="bank")
-        nc.tensor.matmul(out=w_row[:], lhsT=ones[:], rhs=w_blocks[:], start=True, stop=True)
         weigh(ABS_BANKS * BANK, PIXELS, 1.0, 1)
-        w_sum = keep.tile([P, P], F32)
-        nc.vector.tensor_copy(out=w_sum[:], in_=w_row[:])
-        product_sum = keep.tile([P, 1], F32)
-        nc.vector.tensor_tensor(
-            out=product_sum[:], in0=product_sums[:, 0:1], in1=product_sums[:, 1:2], op=ALU.add
-        )
-        size_sum = keep.tile([P, 1], F32)
-        nc.vector.tensor_reduce(
-            out=size_sum[:], in_=size_sums[:], axis=mybir.AxisListType.X, op=ALU.add
-        )
-        without_log = keep.tile([P, 1], F32)
-        nc.vector.scalar_tensor_tensor(
-            out=without_log[:],
-            in0=size_sum[:],
-            scalar=-0.5,
-            in1=product_sum[:],
-            op0=ALU.mult,
-            op1=ALU.add,
-        )
 
-        repeated = keep.tile([P, P], F32)
-        nc.vector.tensor_scalar(
-            out=repeated[:],
-            in0=ones[:],
-            scalar1=without_log[:, 0:1],
-            scalar2=log_sum[:, 0:1],
-            op0=ALU.mult,
-            op1=ALU.subtract,
-        )
-        as_rows = psum.tile([P, P], F32, tag="bank")
-        nc.tensor.transpose(as_rows[:], repeated[:], ident[:])
+        total = psum.tile([P, P], F32, tag="bank")
+        nc.tensor.matmul(out=total[:], lhsT=ones[:], rhs=w_blocks[:], start=True, stop=False)
+        columns = [size_sums[:, i : i + 1] for i in range(ABS_BANKS)]
+        columns += [log_sums[:, 0:1], product_sums[:, 0:1], product_sums[:, 1:2], log_sums[:, 1:2]]
+        for n, column in enumerate(columns):
+            nc.tensor.matmul(
+                out=total[:],
+                lhsT=column.to_broadcast([P, P]),
+                rhs=ident[:],
+                is_transpose=True,
+                start=False,
+                stop=(n == len(columns) - 1),
+            )
         result = keep.tile([P, P], F32)
-        nc.vector.tensor_tensor(out=result[:], in0=as_rows[:], in1=w_sum[:], op=ALU.add)
+        nc.vector.tensor_scalar(
+            out=result[:], in0=total[:], scalar1=-1.0, scalar2=None, op0=ALU.mult
+        )
         nc.sync.dma_start(out=out.rearrange("(o b) -> o b", o=1), in_=result[0:1, :])

@@ -27,7 +27,7 @@ LIVE_ROWS = 4
 SOFTPLUS_CAP = 20.0
 EARLY_BANKS = 2
 N_PAIRS = 2
-ABS_BANKS = 2
+ABS_BANKS = 3
 FP4_WORD_BYTES = 2
 MX_ALIGN = 64
 
@@ -108,23 +108,27 @@ def tile_gmvae_pb_s_kernel(
         nc.tensor.matmul(out=b2_spread[:], lhsT=ones_bf16[:], rhs=b2_row[:], start=True, stop=True)
         b2 = keep.tile([P, HIDDEN], F32)
         nc.scalar.copy(out=b2[:], in_=b2_spread[:])
-        z2 = psum.tile([P, HIDDEN], F32, tag="bank")
-        nc.tensor.matmul_mx(
-            out=z2[:],
-            lhsT=h1_codes[:].bitcast(FP8X4),
-            lhsT_scale=h1_plane[:],
-            rhs=w2_words[:].bitcast(FP4X4),
-            rhs_scale=w2_plane[:],
-            start=True,
-            stop=True,
-        )
+        halves = (slice(0, HIDDEN // 2), slice(HIDDEN // 2, HIDDEN))
+        z2 = []
+        for n, cols in enumerate(halves):
+            z2.append(psum.tile([P, HIDDEN // 2], F32, tag="bank", name="z2_%d" % n))
+            nc.tensor.matmul_mx(
+                out=z2[n][:],
+                lhsT=h1_codes[:].bitcast(FP8X4),
+                lhsT_scale=h1_plane[:],
+                rhs=w2_words[
+                    :, FP4_WORD_BYTES * cols.start : FP4_WORD_BYTES * cols.stop
+                ].bitcast(FP4X4),
+                rhs_scale=w2_plane[:, cols],
+                start=True,
+                stop=True,
+            )
         v2 = keep.tile([P, HIDDEN], F32)
         exp_v2 = keep.tile([P, HIDDEN], F32)
         relu_less_1 = keep.tile([P, HIDDEN], F32)
         d2 = keep.tile([P, HIDDEN], BF16)
-        halves = (slice(0, HIDDEN // 2), slice(HIDDEN // 2, HIDDEN))
-        for cols in halves:
-            nc.vector.tensor_tensor(out=v2[:, cols], in0=z2[:, cols], in1=b2[:, cols], op=ALU.add)
+        for n, cols in enumerate(halves):
+            nc.vector.tensor_tensor(out=v2[:, cols], in0=z2[n][:], in1=b2[:, cols], op=ALU.add)
             nc.scalar.activation(out=exp_v2[:, cols], in_=v2[:, cols], func=ACT.Exp)
         for cols in halves:
             nc.vector.tensor_scalar(
@@ -146,17 +150,17 @@ def tile_gmvae_pb_s_kernel(
             )
 
         d2_codes, d2_plane = quantise_rows(nc, psum, keep, ident[:], d2[:], "d2")
-        z3 = []
-        for i in range(N_BANKS):
-            z3.append(psum.tile([P, BANK], F32, tag="bank", name="z3_%d" % i))
+        pieces = [(0, BANK // 2), (BANK // 2, BANK)]
+        pieces += [(i * BANK, (i + 1) * BANK) for i in range(1, N_BANKS)]
+        z3 = {}
+        for first, last in pieces:
+            z3[first] = psum.tile([P, last - first], F32, tag="bank", name="z3_%d" % first)
             nc.tensor.matmul_mx(
-                out=z3[i][:],
+                out=z3[first][:],
                 lhsT=d2_codes[:].bitcast(FP8X4),
                 lhsT_scale=d2_plane[:],
-                rhs=w3_words[
-                    :, FP4_WORD_BYTES * i * BANK : FP4_WORD_BYTES * (i + 1) * BANK
-                ].bitcast(FP4X4),
-                rhs_scale=w3_plane[:, i * BANK : (i + 1) * BANK],
+                rhs=w3_words[:, FP4_WORD_BYTES * first : FP4_WORD_BYTES * last].bitcast(FP4X4),
+                rhs_scale=w3_plane[:, first:last],
                 start=True,
                 stop=True,
             )
@@ -164,53 +168,51 @@ def tile_gmvae_pb_s_kernel(
         minus_v = keep.tile([P, PIXELS], F32)
         clipped = keep.tile([P, PIXELS], F32)
         growth = keep.tile([P, PIXELS], F32)
-        size_sums = keep.tile([P, ABS_BANKS], F32)
+        abs_pieces = [p for p in pieces if p[1] <= ABS_BANKS * BANK]
+        size_sums = keep.tile([P, len(abs_pieces)], F32)
 
         def bank(i):
             return slice(i * BANK, (i + 1) * BANK)
 
-        def add_bias(i):
+        def add_bias(first, last):
             nc.vector.scalar_tensor_tensor(
-                out=minus_v[:, bank(i)],
-                in0=z3[i][:],
+                out=minus_v[:, first:last],
+                in0=z3[first][:],
                 scalar=-1.0,
-                in1=b3[:, bank(i)],
+                in1=b3[:, first:last],
                 op0=ALU.mult,
                 op1=ALU.subtract,
             )
 
-        def exp_of_size(i):
-            nc.scalar.activation(
-                out=clipped[:, bank(i)],
-                in_=minus_v[:, bank(i)],
-                func=ACT.Abs,
-                scale=0.5,
-                accum_out=size_sums[:, i : i + 1],
-            )
-            nc.scalar.activation(
-                out=growth[:, bank(i)], in_=clipped[:, bank(i)], func=ACT.Exp, scale=-2.0
-            )
-
-        def exp_of_cap(i):
-            nc.vector.tensor_scalar(
-                out=clipped[:, bank(i)],
-                in0=minus_v[:, bank(i)],
-                scalar1=-SOFTPLUS_CAP,
-                scalar2=None,
-                op0=ALU.max,
-            )
-            nc.scalar.activation(
-                out=growth[:, bank(i)], in_=clipped[:, bank(i)], func=ACT.Exp, scale=-1.0
-            )
-
-        add_bias(0)
-        for i in range(N_BANKS):
-            if i + 1 < N_BANKS:
-                add_bias(i + 1)
-            if i < ABS_BANKS:
-                exp_of_size(i)
+        def clip(n):
+            first, last = pieces[n]
+            if n < len(abs_pieces):
+                nc.scalar.activation(
+                    out=clipped[:, first:last],
+                    in_=minus_v[:, first:last],
+                    func=ACT.Abs,
+                    scale=0.5,
+                    accum_out=size_sums[:, n : n + 1],
+                )
+                factor = -2.0
             else:
-                exp_of_cap(i)
+                nc.vector.tensor_scalar(
+                    out=clipped[:, first:last],
+                    in0=minus_v[:, first:last],
+                    scalar1=-SOFTPLUS_CAP,
+                    scalar2=None,
+                    op0=ALU.max,
+                )
+                factor = -1.0
+            nc.scalar.activation(
+                out=growth[:, first:last], in_=clipped[:, first:last], func=ACT.Exp, scale=factor
+            )
+
+        add_bias(*pieces[0])
+        for n in range(len(pieces)):
+            if n + 1 < len(pieces):
+                add_bias(*pieces[n + 1])
+            clip(n)
 
         w_turned = psum.tile([P, P], F32, tag="bank")
         first_block, blocks = ABS_BANKS * BANK // P, PIXELS // P
@@ -277,7 +279,7 @@ def tile_gmvae_pb_s_kernel(
 
         total = psum.tile([P, P], F32, tag="bank")
         nc.tensor.matmul(out=total[:], lhsT=ones[:], rhs=w_blocks[:], start=True, stop=False)
-        columns = [size_sums[:, i : i + 1] for i in range(ABS_BANKS)]
+        columns = [size_sums[:, i : i + 1] for i in range(len(abs_pieces))]
         columns += [log_sums[:, 0:1], product_sums[:, 0:1], product_sums[:, 1:2], log_sums[:, 1:2]]
         for n, column in enumerate(columns):
             nc.tensor.matmul(

from contextlib import ExitStack

import concourse.mybir as mybir
from concourse.masks import make_identity

F32 = mybir.dt.float32
BF16 = mybir.dt.bfloat16
I32 = mybir.dt.int32
U8 = mybir.dt.uint8
U32 = mybir.dt.uint32
FP8X4 = mybir.dt.float8_e4m3fn_x4
FP4X4 = mybir.dt.float4_e2m1fn_x4
ALU = mybir.AluOpType
ACT = mybir.ActivationFunctionType

P = 128
HIDDEN = 512
PIXELS = 3584
BANK = 512
N_BANKS = PIXELS // BANK
assert N_BANKS % 2 == 1
PACK = 4
PAIRS = PACK // 2
QUADRANTS = 4
QUADRANT = P // QUADRANTS
LIVE_ROWS = 4
SOFTPLUS_CAP = 20.0
EARLY_BANKS = 2
N_PAIRS = 2
ABS_BANKS = 3
FP4_WORD_BYTES = 2
MX_ALIGN = 64

FLOPS = 2 * P * HIDDEN * (HIDDEN + PIXELS)


def load_scale_rows(nc, plane, scales):
    for quadrant in range(QUADRANTS):
        first = QUADRANT * quadrant
        nc.sync.dma_start(
            out=plane[first : first + LIVE_ROWS, :].bitcast(I32),
            in_=scales[LIVE_ROWS * quadrant : LIVE_ROWS * (quadrant + 1), :].bitcast(I32),
        )


def quantise_rows(nc, psum, keep, ident, rows, name):
    words = rows.bitcast(F32)
    turned = psum.tile([P, PAIRS, P], F32, tag="bank", name=name + "_turned")
    for u in range(PAIRS):
        nc.tensor.transpose(turned[:, u, :], words[:, u : HIDDEN // 2 : PAIRS], ident)
    grouped = keep.tile([P, PACK * P], BF16, align_bytes=MX_ALIGN, name=name + "_grouped")
    nc.scalar.copy(
        out=grouped[:].bitcast(F32).rearrange("p (b u) -> p b u", u=PAIRS),
        in_=turned[:].rearrange("p u b -> p b u"),
    )
    codes = keep.tile([P, P], U32, align_bytes=MX_ALIGN, name=name + "_codes")
    plane = keep.tile([P, P], U8, align_bytes=MX_ALIGN, name=name + "_plane")
    nc.vector.quantize_mx(out=codes[:].bitcast(FP8X4), scales=plane[:], in_=grouped[:])
    return codes, plane


def tile_gmvae_pb_s_kernel(
    tc, dec_h1, x, dw2_words, dw2_scales, db2, dw3_words, dw3_scales, db3, out
):
    nc = tc.nc
    with ExitStack() as ctx:
        ctx.enter_context(tc.manual_schedule())
        keep = ctx.enter_context(tc.tile_pool(name="keep", bufs=1))
        psum = ctx.enter_context(tc.psum_pool(name="psum", bufs=8))

        b2_row = keep.tile([P, HIDDEN], BF16)
        nc.vector.memset(b2_row[:], 0.0)
        w2_plane = keep.tile([P, HIDDEN], U8, align_bytes=MX_ALIGN)
        w3_plane = keep.tile([P, PIXELS], U8, align_bytes=MX_ALIGN)
        nc.vector.memset(w2_plane[:].bitcast(I32), 0)
        nc.vector.memset(w3_plane[:].bitcast(I32), 0)

        ident = keep.tile([P, P], F32)
        make_identity(nc, ident[:])
        ones = keep.tile([P, P], F32)
        nc.vector.memset(ones[:], 1.0)
        ones_bf16 = keep.tile([P, P], BF16)
        nc.vector.memset(ones_bf16[:], 1.0)

        h1 = keep.tile([P, HIDDEN], BF16)
        nc.sync.dma_start(out=h1[:], in_=dec_h1)
        nc.sync.dma_start(out=b2_row[0:1, :], in_=db2.rearrange("(o h) -> o h", o=1))
        load_scale_rows(nc, w2_plane, dw2_scales[0])
        w2_words = keep.tile([P, FP4_WORD_BYTES * HIDDEN], U8, align_bytes=MX_ALIGN)
        nc.sync.dma_start(out=w2_words[:].bitcast(I32), in_=dw2_words[0].bitcast(I32))
        load_scale_rows(nc, w3_plane, dw3_scales[0])
        w3_words = keep.tile([P, FP4_WORD_BYTES * PIXELS], U8, align_bytes=MX_ALIGN)
        w3_early = slice(0, FP4_WORD_BYTES * EARLY_BANKS * BANK)
        w3_late = slice(FP4_WORD_BYTES * EARLY_BANKS * BANK, FP4_WORD_BYTES * PIXELS)
        nc.sync.dma_start(
            out=w3_words[:, w3_early].bitcast(I32), in_=dw3_words[0][:, w3_early].bitcast(I32)
        )
        b3 = keep.tile([P, PIXELS], BF16)
        nc.sync.dma_start(out=b3[:], in_=db3.partition_broadcast(P))
        nc.sync.dma_start(
            out=w3_words[:, w3_late].bitcast(I32), in_=dw3_words[0][:, w3_late].bitcast(I32)
        )
        x_sb = keep.tile([P, PIXELS], BF16)
        nc.sync.dma_start(out=x_sb[:], in_=x)

        h1_codes, h1_plane = quantise_rows(nc, psum, keep, ident[:], h1[:], "h1")
        b2_spread = psum.tile([P, HIDDEN], F32, tag="bank")
        nc.tensor.matmul(out=b2_spread[:], lhsT=ones_bf16[:], rhs=b2_row[:], start=True, stop=True)
        b2 = keep.tile([P, HIDDEN], F32)
        nc.scalar.copy(out=b2[:], in_=b2_spread[:])
        halves = (slice(0, HIDDEN // 2), slice(HIDDEN // 2, HIDDEN))
        z2 = []
        for n, cols in enumerate(halves):
            z2.append(psum.tile([P, HIDDEN // 2], F32, tag="bank", name="z2_%d" % n))
            nc.tensor.matmul_mx(
                out=z2[n][:],
                lhsT=h1_codes[:].bitcast(FP8X4),
                lhsT_scale=h1_plane[:],
                rhs=w2_words[
                    :, FP4_WORD_BYTES * cols.start : FP4_WORD_BYTES * cols.stop
                ].bitcast(FP4X4),
                rhs_scale=w2_plane[:, cols],
                start=True,
                stop=True,
            )
        v2 = keep.tile([P, HIDDEN], F32)
        exp_v2 = keep.tile([P, HIDDEN], F32)
        relu_less_1 = keep.tile([P, HIDDEN], F32)
        d2 = keep.tile([P, HIDDEN], BF16)
        for n, cols in enumerate(halves):
            nc.vector.tensor_tensor(out=v2[:, cols], in0=z2[n][:], in1=b2[:, cols], op=ALU.add)
            nc.scalar.activation(out=exp_v2[:, cols], in_=v2[:, cols], func=ACT.Exp)
        for cols in halves:
            nc.vector.tensor_scalar(
                out=relu_less_1[:, cols],
                in0=v2[:, cols],
                scalar1=0.0,
                scalar2=-1.0,
                op0=ALU.max,
                op1=ALU.add,
            )
        for cols in halves:
            nc.vector.scalar_tensor_tensor(
                out=d2[:, cols],
                in0=exp_v2[:, cols],
                scalar=1.0,
                in1=relu_less_1[:, cols],
                op0=ALU.min,
                op1=ALU.add,
            )

        d2_codes, d2_plane = quantise_rows(nc, psum, keep, ident[:], d2[:], "d2")
        pieces = [(0, BANK // 2), (BANK // 2, BANK)]
        pieces += [(i * BANK, (i + 1) * BANK) for i in range(1, N_BANKS)]
        z3 = {}
        for first, last in pieces:
            z3[first] = psum.tile([P, last - first], F32, tag="bank", name="z3_%d" % first)
            nc.tensor.matmul_mx(
                out=z3[first][:],
                lhsT=d2_codes[:].bitcast(FP8X4),
                lhsT_scale=d2_plane[:],
                rhs=w3_words[:, FP4_WORD_BYTES * first : FP4_WORD_BYTES * last].bitcast(FP4X4),
                rhs_scale=w3_plane[:, first:last],
                start=True,
                stop=True,
            )

        minus_v = keep.tile([P, PIXELS], F32)
        clipped = keep.tile([P, PIXELS], F32)
        growth = keep.tile([P, PIXELS], F32)
        abs_pieces = [p for p in pieces if p[1] <= ABS_BANKS * BANK]
        size_sums = keep.tile([P, len(abs_pieces)], F32)

        def bank(i):
            return slice(i * BANK, (i + 1) * BANK)

        def add_bias(first, last):
            nc.vector.scalar_tensor_tensor(
                out=minus_v[:, first:last],
                in0=z3[first][:],
                scalar=-1.0,
                in1=b3[:, first:last],
                op0=ALU.mult,
                op1=ALU.subtract,
            )

        def clip(n):
            first, last = pieces[n]
            if n < len(abs_pieces):
                nc.scalar.activation(
                    out=clipped[:, first:last],
                    in_=minus_v[:, first:last],
                    func=ACT.Abs,
                    scale=0.5,
                    accum_out=size_sums[:, n : n + 1],
                )
                factor = -2.0
            else:
                nc.vector.tensor_scalar(
                    out=clipped[:, first:last],
                    in0=minus_v[:, first:last],
                    scalar1=-SOFTPLUS_CAP,
                    scalar2=None,
                    op0=ALU.max,
                )
                factor = -1.0
            nc.scalar.activation(
                out=growth[:, first:last], in_=clipped[:, first:last], func=ACT.Exp, scale=factor
            )

        add_bias(*pieces[0])
        for n in range(len(pieces)):
            if n + 1 < len(pieces):
                add_bias(*pieces[n + 1])
            clip(n)

        w_turned = psum.tile([P, P], F32, tag="bank")
        first_block, blocks = ABS_BANKS * BANK // P, PIXELS // P
        for n in range(first_block, blocks):
            nc.tensor.matmul(
                out=w_turned[:],
                lhsT=clipped[:, n * P : (n + 1) * P],
                rhs=ident[:],
                is_transpose=True,
                start=(n == first_block),
                stop=(n == blocks - 1),
            )

        pair_products = keep.tile([P, N_PAIRS * BANK], F32)
        plus_one = keep.tile([P, N_PAIRS * BANK], F32)
        for j in range(N_PAIRS):
            nc.vector.tensor_scalar(
                out=plus_one[:, bank(j)],
                in0=growth[:, bank(2 * j)],
                scalar1=1.0,
                scalar2=None,
                op0=ALU.add,
            )
        for j in range(N_PAIRS):
            nc.vector.scalar_tensor_tensor(
                out=pair_products[:, bank(j)],
                in0=growth[:, bank(2 * j + 1)],
                scalar=1.0,
                in1=plus_one[:, bank(j)],
                op0=ALU.add,
                op1=ALU.mult,
            )

        log_sums = keep.tile([P, 2], F32)
        single = slice(2 * N_PAIRS * BANK, PIXELS)
        nc.scalar.activation(
            out=growth[:, single],
            in_=growth[:, single],
            func=ACT.Ln,
            bias=1.0,
            accum_out=log_sums[:, 0:1],
        )
        nc.scalar.activation(
            out=pair_products[:], in_=pair_products[:], func=ACT.Ln, accum_out=log_sums[:, 1:2]
        )
        product = keep.tile([P, PIXELS], F32)
        product_sums = keep.tile([P, 2], F32)

        def weigh(first, last, middle, j):
            nc.vector.scalar_tensor_tensor(
                out=product[:, first:last],
                in0=x_sb[:, first:last],
                scalar=middle,
                in1=minus_v[:, first:last],
                op0=ALU.subtract,
                op1=ALU.mult,
                accum_out=product_sums[:, j : j + 1],
            )

        weigh(0, ABS_BANKS * BANK, 0.5, 0)
        w_blocks = keep.tile([P, P], F32)
        nc.vector.tensor_copy(out=w_blocks[:], in_=w_turned[:])
        weigh(ABS_BANKS * BANK, PIXELS, 1.0, 1)

        total = psum.tile([P, P], F32, tag="bank")
        nc.tensor.matmul(out=total[:], lhsT=ones[:], rhs=w_blocks[:], start=True, stop=False)
        columns = [size_sums[:, i : i + 1] for i in range(len(abs_pieces))]
        columns += [log_sums[:, 0:1], product_sums[:, 0:1], product_sums[:, 1:2], log_sums[:, 1:2]]
        for n, column in enumerate(columns):
            nc.tensor.matmul(
                out=total[:],
                lhsT=column.to_broadcast([P, P]),
                rhs=ident[:],
                is_transpose=True,
                start=False,
                stop=(n == len(columns) - 1),
            )
        result = keep.tile([P, P], F32)
        nc.vector.tensor_scalar(
            out=result[:], in0=total[:], scalar1=-1.0, scalar2=None, op0=ALU.mult
        )
        nc.sync.dma_start(out=out.rearrange("(o b) -> o b", o=1), in_=result[0:1, :])
